import numpy as np
import ml_dtypes


def mxq(x, axis, fmt="e4m3"):
    dtype, down = {"e4m3": (ml_dtypes.float8_e4m3fn, 7), "e5m2": (ml_dtypes.float8_e5m2, 14)}[fmt]
    v = np.moveaxis(np.asarray(x, np.float32).astype(ml_dtypes.bfloat16).astype(np.float64), axis, -1)
    blocks = v.reshape(v.shape[:-1] + (-1, 32))
    amax = np.abs(blocks).max(-1, keepdims=True)
    byte = np.maximum(np.where(amax > 0, np.frexp(amax)[1] - 1 + 127, 0) - down, 1)
    scale = np.exp2(byte - 127.0)
    codes = (blocks / scale).astype(np.float32).astype(dtype).astype(np.float64)
    return np.moveaxis((codes * scale).reshape(v.shape), -1, axis)


WIDE = False


def mx_kscale(k):
    if not WIDE:
        return np.ones(k)
    levels = np.array([18, -18])
    if k % 512:
        return np.exp2(np.random.permutation(np.resize(levels, k // 32))).repeat(32)
    a = np.empty((k // 512, 16))
    for p in range(k // 512):
        a[p, :8] = np.random.permutation(np.resize(levels, 8))
        for g in range(8):
            far = levels[np.abs(levels - a[p, g]) >= 10]
            a[p, g + 8] = far[np.random.randint(len(far))]
    return np.exp2(a.ravel()).repeat(32)


BF16 = ml_dtypes.bfloat16


def bf(x):
    return np.asarray(x, np.float32).astype(BF16)


def f64(x):
    return np.asarray(x).astype(np.float64)


B, L, E, DV = 2, 1024, 128, 1024


def valid_keys(mask):
    return np.maximum(np.sum(~mask, axis=-1, keepdims=True), 1).astype(np.float64)


def setup_inputs():
    s = mx_kscale(L)[None, :, None]
    w = mx_kscale(DV)[None, None, :]
    c = mx_kscale(L)[None, :, None]
    u = bf(np.random.standard_normal((B, L, DV)))
    q0 = bf(np.random.standard_normal((B, L, E)))
    k0 = bf(np.random.standard_normal((B, L, E)))
    v0 = bf(np.random.standard_normal((B, L, DV)) * np.sqrt(np.sqrt(L)))
    attn_mask = np.random.random_sample((B, L, L)) < 0.25
    g = bf(np.random.standard_normal((B, L, DV)) * np.exp2(np.random.randint(-6, 1, (B, L, 1))) * 16.0 / s * w)
    scores = f64(q0) @ f64(k0).transpose(0, 2, 1)
    return {"u": u, "q": bf(f64(q0) * s), "k": bf(f64(k0) / c), "v": bf(f64(v0) * c / w), "attn_mask": attn_mask, "scores": np.asarray(scores, np.float32), "grad_out": g}


def reference(u, q, k, v, attn_mask, scores, grad_out):
    mask = np.asarray(attn_mask).astype(bool)
    scale = 1.0 / np.sqrt(q.shape[-1])
    dz2 = f64(grad_out) * f64(u)
    dA = mxq(dz2, 2, "e5m2") @ mxq(f64(v), 2, "e4m3").transpose(0, 2, 1)
    r = np.where(mask, 0.0, np.maximum(scale * f64(scores), 0.0))
    dS = dA * (2.0 * scale * r / valid_keys(mask))
    dq = mxq(dS, 2, "e5m2") @ mxq(f64(k), 1, "e4m3")
    dk = mxq(dS, 1, "e5m2").transpose(0, 2, 1) @ mxq(f64(q), 1, "e4m3")
    return dq, dk

@@ -1,0 +1,413 @@
+from contextlib import ExitStack
+
+import concourse.mybir as mybir
+from concourse.masks import make_identity
+
+B, L, E, DV = 2, 1024, 128, 1024
+FLOPS = 2 * B * L * L * DV + 2 * 2 * B * L * L * E
+
+F32 = mybir.dt.float32
+BF16 = mybir.dt.bfloat16
+I32 = mybir.dt.int32
+U32 = mybir.dt.uint32
+U8 = mybir.dt.uint8
+E4M3 = mybir.dt.float8_e4m3fn_x4
+E5M2 = mybir.dt.float8_e5m2_x4
+ALU = mybir.AluOpType
+ACT = mybir.ActivationFunctionType
+
+P = 128
+PACK = 4
+PASS = P * PACK
+PASSES = L // PASS
+BANK = 512
+STEPS = B * L // P
+STEPS_B = L // P
+Q_COLS = 256
+QUARTERS = L // Q_COLS
+KQ_BLOCKS = 7
+
+
+def tile_gateattention_v_kernel(tc, u, q, k, v, attn_mask, scores, grad_out, out_0, out_1):
+    nc = tc.nc
+    mask_words = attn_mask.bitcast(I32)
+
+    with ExitStack() as ctx:
+        ctx.enter_context(tc.manual_schedule())
+        keep = ctx.enter_context(tc.tile_pool(name="keep", bufs=1))
+        pool = ctx.enter_context(tc.tile_pool(name="work", bufs=2))
+        ps_tr = ctx.enter_context(tc.psum_pool(name="ps_tr", bufs=3))
+        ps_da = ctx.enter_context(tc.psum_pool(name="ps_da", bufs=2))
+        ps_o = ctx.enter_context(tc.psum_pool(name="ps_o", bufs=3))
+
+        ident = keep.tile([P, P], F32, name="ident")
+        make_identity(nc, ident[:])
+        count = keep.tile([P, STEPS], F32, name="count")
+        divisor = keep.tile([P, STEPS], F32, name="divisor")
+        factor = keep.tile([P, STEPS], F32, name="factor")
+
+        v_codes, v_scales, kq_codes, kq_scales = {}, {}, {}, {}
+        for b in range(B):
+            v_codes[b] = keep.tile([P, PASSES, L], U32, name="v_codes" + str(b), align_bytes=64)
+            v_scales[b] = keep.tile([P, PASSES, L], U8, name="v_scales" + str(b), align_bytes=64)
+            kq_codes[b] = keep.tile([P, KQ_BLOCKS * E], U32, name="kq_codes" + str(b), align_bytes=64)
+            kq_scales[b] = keep.tile([P, KQ_BLOCKS * E], U8, name="kq_scales" + str(b), align_bytes=64)
+            nc.gpsimd.memset(kq_codes[b][:, 4 * E :], 0)
+            nc.gpsimd.memset(kq_scales[b][:, 4 * E :], 0)
+
+        v_raw, u_raw, g_raw, kq_raw, mask_raw, s_raw = {}, {}, {}, {}, {}, {}
+        dz, dz_codes, shown, weight, dS = {}, {}, {}, {}, {}
+        vt, turned, dsb_codes, stage_0, stage_1, banks = {}, {}, {}, {}, {}, {}
+
+        def place(s):
+            b, r = divmod(s, STEPS_B)
+            g, j = divmod(r, PACK)
+            return b, g, j
+
+        def rows_of(x, s):
+            b, g, j = place(s)
+            return x[b, g * PASS : (g + 1) * PASS, :].rearrange("(p j) c -> p j c", j=PACK)
+
+        def load_v(b, c):
+            t = pool.tile([P, 2, DV], BF16, tag="v_raw", name="v_raw", bufs=4)
+            nc.sync.dma_start(out=t[:], in_=v[b, c * Q_COLS : (c + 1) * Q_COLS, :].rearrange("(p a) d -> p a d", a=2))
+            v_raw[b, c] = t
+
+        def load_ug(pair):
+            s = 2 * pair
+            b, g, j = place(s)
+            tg = pool.tile([P, 2, DV], BF16, tag="g_raw", name="g_raw", bufs=3)
+            nc.sync.dma_start(out=tg[:], in_=rows_of(grad_out, s)[:, j : j + 2, :])
+            tu = pool.tile([P, 2, DV], BF16, tag="u_raw", name="u_raw", bufs=3)
+            nc.sync.dma_start(out=tu[:], in_=rows_of(u, s)[:, j : j + 2, :])
+            g_raw[pair], u_raw[pair] = tg, tu
+
+        def load_kq(b):
+            tk = pool.tile([P, PASSES, PACK, E], BF16, tag="k_raw", name="k_raw", bufs=1)
+            nc.sync.dma_start(out=tk[:], in_=k[b].rearrange("(g p j) e -> p g j e", p=P, j=PACK))
+            tq = pool.tile([P, PASSES, PACK, E], BF16, tag="q_raw", name="q_raw", bufs=1)
+            nc.sync.dma_start(out=tq[:], in_=q[b].rearrange("(g p j) e -> p g j e", p=P, j=PACK))
+            kq_raw[b] = (tk, tq)
+
+        def load_mask(s):
+            j = place(s)[2]
+            t = pool.tile([P, 2 * L], I32, tag="mask", name="mask", bufs=4)
+            nc.sync.dma_start(out=t[:], in_=rows_of(mask_words, s)[:, j, :])
+            mask_raw[s] = t
+
+        def load_scores(s, pieces):
+            j = place(s)[2]
+            t = pool.tile([P, L], F32, tag="scores", name="scores", bufs=4)
+            n = L // pieces
+            for h in range(pieces):
+                nc.sync.dma_start(out=t[:, h * n : (h + 1) * n], in_=rows_of(scores, s)[:, j, h * n : (h + 1) * n])
+            s_raw[s] = t
+
+        def turn_v(b, c):
+            words = v_raw[b, c][:].bitcast(F32)
+            for g in range(PASSES):
+                bank = ps_tr.tile([P, 2, 2, P], F32, tag="tr", name="bank_v")
+                for w in range(2):
+                    for a in range(2):
+                        nc.tensor.transpose(bank[:, w, a, :], words[:, a, 2 * P * g + w : 2 * P * (g + 1) : 2], ident[:])
+                banks["v", b, c, g] = bank
+
+        def copy_v(b, c):
+            for g in range(PASSES):
+                t = pool.tile([P, PACK * Q_COLS], BF16, tag="turned", name="vt", bufs=6, align_bytes=64)
+                nc.scalar.copy(
+                    out=t[:].bitcast(F32).rearrange("p (r a w) -> p r a w", a=2, w=2),
+                    in_=banks["v", b, c, g][:].rearrange("p w a r -> p r a w"),
+                )
+                vt[b, c, g] = t
+
+        def quant_v(b, c):
+            cols = slice(c * Q_COLS, (c + 1) * Q_COLS)
+            for g in range(PASSES):
+                nc.vector.quantize_mx(out=v_codes[b][:, g, cols].bitcast(E4M3), scales=v_scales[b][:, g, cols], in_=vt[b, c, g][:])
+
+        def prep_kq(b):
+            parts = []
+            for raw in kq_raw[b]:
+                t = pool.tile([P, PACK * Q_COLS], BF16, tag="turned", name="kqt", bufs=6, align_bytes=64)
+                nc.vector.tensor_copy(
+                    out=t[:].rearrange("p (g e j) -> p g e j", g=PASSES, j=PACK), in_=raw[:].rearrange("p g j e -> p g e j")
+                )
+                parts.append(t)
+            for i, t in enumerate(parts):
+                cols = slice(i * PASSES * E, (i + 1) * PASSES * E)
+                nc.vector.quantize_mx(out=kq_codes[b][:, cols].bitcast(E4M3), scales=kq_scales[b][:, cols], in_=t[:])
+
+        def product(s):
+            jj = s % 2
+            t = pool.tile([P, DV], BF16, tag="dz", name="dz", bufs=3)
+            nc.vector.tensor_tensor(out=t[:], in0=g_raw[s // 2][:, jj, :], in1=u_raw[s // 2][:, jj, :], op=ALU.mult)
+            dz[s] = t
+
+        def turn_rows(kind, s, tile):
+            words = tile.bitcast(F32)
+            bank = ps_tr.tile([P, PASSES, 2, P], F32, tag="tr", name="bank_t")
+            for g in range(PASSES):
+                for w in range(2):
+                    nc.tensor.transpose(bank[:, g, w, :], words[:, 2 * P * g + w : 2 * P * (g + 1) : 2], ident[:])
+            banks[kind, s] = bank
+
+        def copy_rows(kind, s):
+            t = pool.tile([P, PACK * Q_COLS], BF16, tag="turned", name="rt", bufs=6, align_bytes=64)
+            nc.scalar.copy(
+                out=t[:].bitcast(F32).rearrange("p (g r w) -> p g r w", g=PASSES, w=2),
+                in_=banks[kind, s][:].rearrange("p g w r -> p g r w"),
+            )
+            turned[kind, s] = t
+
+        def quant_rows(kind, s):
+            c = pool.tile([P, PASSES * P], U32, tag="rows_codes", name="rows_codes", bufs=5, align_bytes=64)
+            e = pool.tile([P, PASSES * P], U8, tag="rows_scales", name="rows_scales", bufs=5, align_bytes=64)
+            nc.vector.quantize_mx(out=c[:].bitcast(E5M2), scales=e[:], in_=turned[kind, s][:])
+            dz_codes[kind, s] = (c, e)
+
+        def multiply_a(s):
+            b = place(s)[0]
+            c, e = dz_codes["dz", s]
+            for h in range(L // BANK):
+                bank = ps_da.tile([P, BANK], F32, tag="da", name="bank_a")
+                cols = slice(h * BANK, (h + 1) * BANK)
+                for g in range(PASSES):
+                    mine = slice(g * P, (g + 1) * P)
+                    nc.tensor.matmul_mx(
+                        out=bank[:],
+                        lhsT=c[:, mine].bitcast(E5M2),
+                        lhsT_scale=e[:, mine],
+                        rhs=v_codes[b][:, g, cols].bitcast(E4M3),
+                        rhs_scale=v_scales[b][:, g, cols],
+                        start=(g == 0),
+                        stop=(g == PASSES - 1),
+                    )
+                banks["da", s, h] = bank
+
+        def show(s):
+            t = pool.tile([P, L], BF16, tag="shown", name="shown", bufs=3)
+            low = mask_raw[s][:].bitcast(U32).rearrange("p (n w) -> p n w", w=2)[:, :, 0]
+            nc.scalar.activation(out=t[:], in_=low, func=ACT.Copy, scale=-1.0, bias=1.0, accum_out=count[:, s : s + 1])
+            shown[s] = t
+
+        def factor_1(s):
+            nc.vector.tensor_scalar(
+                out=divisor[:, s : s + 1], in0=count[:, s : s + 1], scalar1=1.0, scalar2=64.0, op0=ALU.max, op1=ALU.mult
+            )
+
+        def factor_2(s):
+            nc.vector.reciprocal(out=factor[:, s : s + 1], in_=divisor[:, s : s + 1])
+
+        def weigh(s):
+            t = pool.tile([P, L], F32, tag="weight", name="weight", bufs=2)
+            for h in range(L // BANK):
+                cols = slice(h * BANK, (h + 1) * BANK)
+                nc.vector.scalar_tensor_tensor(
+                    out=t[:, cols], in0=s_raw[s][:, cols], scalar=0.0, in1=shown[s][:, cols], op0=ALU.max, op1=ALU.mult
+                )
+            weight[s] = t
+
+        def grad_s(s):
+            b, g, j = place(s)
+            if j == 0:
+                t = pool.tile([P, PACK, L], BF16, tag="dS", name="dS", bufs=2)
+                dS[b, g] = t
+            for h in range(L // BANK):
+                cols = slice(h * BANK, (h + 1) * BANK)
+                nc.vector.scalar_tensor_tensor(
+                    out=dS[b, g][:, j, cols],
+                    in0=banks["da", s, h][:],
+                    scalar=factor[:, s : s + 1],
+                    in1=weight[s][:, cols],
+                    op0=ALU.mult,
+                    op1=ALU.mult,
+                )
+
+        def multiply_0(s):
+            b, gm, j = place(s)
+            c, e = dz_codes["ds", s]
+            bank = ps_o.tile([P, BANK], F32, tag="o", name="bank_0")
+            for g in range(PASSES):
+                mine = slice(g * P, (g + 1) * P)
+                cols = slice(g * E, g * E + BANK)
+                nc.tensor.matmul_mx(
+                    out=bank[:],
+                    lhsT=c[:, mine].bitcast(E5M2),
+                    lhsT_scale=e[:, mine],
+                    rhs=kq_codes[b][:, cols].bitcast(E4M3),
+                    rhs_scale=kq_scales[b][:, cols],
+                    start=(g == 0),
+                    stop=(g == PASSES - 1),
+                )
+            banks["o0", s] = bank
+
+        def copy_0(s):
+            b, g, j = place(s)
+            if j == 0:
+                t = pool.tile([P, PACK, E], F32, tag="stage_0", name="stage_0", bufs=4)
+                stage_0[b, g] = t
+            nc.scalar.copy(out=stage_0[b, g][:, j, :], in_=banks["o0", s][:, :E])
+
+        def interleave(b, g, quarter, engine_copy):
+            t = pool.tile([P, Q_COLS, PACK], BF16, tag="inter", name="inter", bufs=4, align_bytes=64)
+            cols = slice(quarter * Q_COLS, (quarter + 1) * Q_COLS)
+            engine_copy(
+                out=t[:].rearrange("p (c i) t -> p c t i", i=4),
+                in_=dS[b, g][:, :, cols].rearrange("p t (c i) -> p c t i", i=4),
+            )
+            turned["b", b, g, quarter] = t
+
+        def quant_b(b, g, quarter):
+            if quarter == 0:
+                c = pool.tile([P, L], U32, tag="dsb_codes", name="dsb_codes", bufs=3, align_bytes=64)
+                e = pool.tile([P, L], U8, tag="dsb_scales", name="dsb_scales", bufs=3, align_bytes=64)
+                dsb_codes[b, g] = (c, e)
+            c, e = dsb_codes[b, g]
+            cols = slice(quarter * Q_COLS, (quarter + 1) * Q_COLS)
+            nc.vector.quantize_mx(
+                out=c[:, cols].bitcast(E5M2), scales=e[:, cols], in_=turned["b", b, g, quarter][:].rearrange("p n t -> p (n t)")
+            )
+
+        def multiply_1(b, i, psum, tag):
+            bank = psum.tile([P, BANK], F32, tag=tag, name="bank_1")
+            mine = slice(i * P, (i + 1) * P)
+            for g in range(PASSES):
+                c, e = dsb_codes[b, g]
+                cols = slice((PASSES + g) * E, (PASSES + g) * E + BANK)
+                nc.tensor.matmul_mx(
+                    out=bank[:],
+                    lhsT=c[:, mine].bitcast(E5M2),
+                    lhsT_scale=e[:, mine],
+                    rhs=kq_codes[b][:, cols].bitcast(E4M3),
+                    rhs_scale=kq_scales[b][:, cols],
+                    start=(g == 0),
+                    stop=(g == PASSES - 1),
+                )
+            banks["o1", b, i] = bank
+
+        def copy_1(b, i, engine_copy):
+            if i == 0:
+                t = pool.tile([P, L // P, E], F32, tag="stage_1", name="stage_1", bufs=2)
+                stage_1[b] = t
+            engine_copy(out=stage_1[b][:, i, :], in_=banks["o1", b, i][:, :E])
+
+        def store_0(b, g):
+            nc.sync.dma_start(
+                out=out_0[b, g * PASS : (g + 1) * PASS, :].rearrange("(p j) e -> p j e", j=PACK), in_=stage_0[b, g][:]
+            )
+
+        def store_1(b, first, last):
+            nc.sync.dma_start(
+                out=out_1[b, first * P : last * P, :].rearrange("(i p) e -> p i e", p=P), in_=stage_1[b][:, first:last, :]
+            )
+
+        chunks = L // Q_COLS
+
+        def load_for(s):
+            if s == 0:
+                for c in range(chunks):
+                    load_v(0, c)
+                load_ug(0)
+                load_mask(0)
+                load_ug(1)
+                load_kq(0)
+            if s + 1 < STEPS:
+                load_mask(s + 1)
+            load_scores(s, 2 if s == STEPS - 1 else 1)
+            if 2 <= s < 2 + chunks:
+                load_v(1, s - 2)
+            if s == 6:
+                load_kq(1)
+            if s % 2 == 0 and s // 2 + 2 < STEPS // 2:
+                load_ug(s // 2 + 2)
+
+        load_for(0)
+        for c in range(chunks):
+            turn_v(0, c)
+            copy_v(0, c)
+            quant_v(0, c)
+
+        for i in range(-3, STEPS):
+            if 0 < i + 3 < STEPS:
+                load_for(i + 3)
+            if i == STEPS - 2:
+                store_0(0, 0)
+                store_0(0, 1)
+                store_1(0, 0, L // P)
+                store_0(1, 0)
+
+            back_b, back_g, quarter = place(i - PACK) if i >= PACK else (0, 0, 0)
+
+            if 0 <= i + 1 < STEPS:
+                show(i + 1)
+            if i >= 2:
+                copy_0(i - 2)
+            if STEPS_B < i <= STEPS_B + QUARTERS:
+                for n in range(2):
+                    copy_1(0, 2 * (i - 1 - STEPS_B) + n, nc.scalar.copy)
+            if i >= PACK:
+                interleave(back_b, back_g, quarter, nc.scalar.copy)
+
+            if i >= 0:
+                weigh(i)
+                grad_s(i)
+            if 4 <= i < 4 + chunks:
+                quant_v(1, i - 4)
+
+            if i >= 0:
+                b, g, j = place(i)
+                turn_rows("ds", i, dS[b, g][:, j, :])
+                copy_rows("ds", i)
+            if 0 <= i + 2 < STEPS:
+                turn_rows("dz", i + 2, dz[i + 2][:])
+                copy_rows("dz", i + 2)
+            if 3 <= i < 3 + chunks:
+                turn_v(1, i - 3)
+                copy_v(1, i - 3)
+
+            if 0 <= i + 1 < STEPS:
+                quant_rows("dz", i + 1)
+                multiply_a(i + 1)
+            if i >= 1:
+                quant_rows("ds", i - 1)
+                multiply_0(i - 1)
+            if i >= PACK:
+                quant_b(back_b, back_g, quarter)
+            if STEPS_B <= i < STEPS_B + QUARTERS:
+                for n in range(2):
+                    multiply_1(0, 2 * (i - STEPS_B) + n, ps_o, "o")
+            if 0 <= i + 1 < STEPS:
+                factor_1(i + 1)
+            if 0 <= i + 3 < STEPS:
+                product(i + 3)
+            if 0 <= i + 1 < STEPS:
+                factor_2(i + 1)
+            if i == -1:
+                prep_kq(0)
+            if i == STEPS_B - 1:
+                prep_kq(1)
+
+        last = STEPS - 1
+        copy_0(last - 1)
+        interleave(1, 1, 0, nc.scalar.copy)
+        interleave(1, 1, 1, nc.vector.tensor_copy)
+        quant_b(1, 1, 0)
+        interleave(1, 1, 2, nc.vector.tensor_copy)
+        interleave(1, 1, 3, nc.scalar.copy)
+        quant_b(1, 1, 1)
+        quant_rows("ds", last)
+        quant_b(1, 1, 2)
+        quant_b(1, 1, 3)
+        for i in range(4):
+            multiply_1(1, i, ps_o if i < 2 else ps_da, "o" if i < 2 else "da")
+        multiply_0(last)
+        for i in range(4):
+            copy_1(1, i, nc.scalar.copy if i % 2 else nc.vector.tensor_copy)
+        copy_0(last)
+        store_0(1, 1)
+        store_1(1, 0, 4)
+        for i in range(4, 8):
+            multiply_1(1, i, ps_o if i < 6 else ps_da, "o" if i < 6 else "da")
+            copy_1(1, i, nc.scalar.copy if i % 2 else nc.vector.tensor_copy)
+        store_1(1, 4, 8)

@@ -112,10 +112,11 @@ def tile_gateattention_v_kernel(tc, u, q, k, v, attn_mask, scores, grad_out, out
                         nc.tensor.transpose(bank[:, w, a, :], words[:, a, 2 * P * g + w : 2 * P * (g + 1) : 2], ident[:])
                 banks["v", b, c, g] = bank
 
-        def copy_v(b, c):
+        def copy_v(b, c, second_copy):
             for g in range(PASSES):
                 t = pool.tile([P, PACK * Q_COLS], BF16, tag="turned", name="vt", bufs=6, align_bytes=64)
-                nc.scalar.copy(
+                engine_copy = second_copy if g else nc.scalar.copy
+                engine_copy(
                     out=t[:].bitcast(F32).rearrange("p (r a w) -> p r a w", a=2, w=2),
                     in_=banks["v", b, c, g][:].rearrange("p w a r -> p r a w"),
                 )
@@ -191,13 +192,13 @@ def tile_gateattention_v_kernel(tc, u, q, k, v, attn_mask, scores, grad_out, out
             nc.scalar.activation(out=t[:], in_=low, func=ACT.Copy, scale=-1.0, bias=1.0, accum_out=count[:, s : s + 1])
             shown[s] = t
 
-        def factor_1(s):
-            nc.vector.tensor_scalar(
-                out=divisor[:, s : s + 1], in0=count[:, s : s + 1], scalar1=1.0, scalar2=64.0, op0=ALU.max, op1=ALU.mult
-            )
+        def divide(s):
+            cols = slice(s, s + 1)
+            nc.gpsimd.tensor_scalar(out=divisor[:, cols], in0=count[:, cols], scalar1=1.0, scalar2=64.0, op0=ALU.max, op1=ALU.mult)
 
-        def factor_2(s):
-            nc.vector.reciprocal(out=factor[:, s : s + 1], in_=divisor[:, s : s + 1])
+        def invert(s):
+            cols = slice(s, s + 1)
+            nc.vector.reciprocal(out=factor[:, cols], in_=divisor[:, cols])
 
         def weigh(s):
             t = pool.tile([P, L], F32, tag="weight", name="weight", bufs=2)
@@ -269,145 +270,207 @@ def tile_gateattention_v_kernel(tc, u, q, k, v, attn_mask, scores, grad_out, out
                 out=c[:, cols].bitcast(E5M2), scales=e[:, cols], in_=turned["b", b, g, quarter][:].rearrange("p n t -> p (n t)")
             )
 
-        def multiply_1(b, i, psum, tag):
+        def open_1(b, i, psum, tag):
             bank = psum.tile([P, BANK], F32, tag=tag, name="bank_1")
-            mine = slice(i * P, (i + 1) * P)
-            for g in range(PASSES):
-                c, e = dsb_codes[b, g]
-                cols = slice((PASSES + g) * E, (PASSES + g) * E + BANK)
-                nc.tensor.matmul_mx(
-                    out=bank[:],
-                    lhsT=c[:, mine].bitcast(E5M2),
-                    lhsT_scale=e[:, mine],
-                    rhs=kq_codes[b][:, cols].bitcast(E4M3),
-                    rhs_scale=kq_scales[b][:, cols],
-                    start=(g == 0),
-                    stop=(g == PASSES - 1),
-                )
             banks["o1", b, i] = bank
 
+        def multiply_1(b, i, g):
+            mine = slice(i * P, (i + 1) * P)
+            c, e = dsb_codes[b, g]
+            cols = slice((PASSES + g) * E, (PASSES + g) * E + BANK)
+            nc.tensor.matmul_mx(
+                out=banks["o1", b, i][:],
+                lhsT=c[:, mine].bitcast(E5M2),
+                lhsT_scale=e[:, mine],
+                rhs=kq_codes[b][:, cols].bitcast(E4M3),
+                rhs_scale=kq_scales[b][:, cols],
+                start=(g == 0),
+                stop=(g == PASSES - 1),
+            )
+
+        def stage(b, h):
+            if (b, h) not in stage_1:
+                t = pool.tile([P, PACK, E], F32, tag="stage_1", name="stage_1", bufs=4)
+                stage_1[b, h] = t
+            return stage_1[b, h]
+
         def copy_1(b, i, engine_copy):
-            if i == 0:
-                t = pool.tile([P, L // P, E], F32, tag="stage_1", name="stage_1", bufs=2)
-                stage_1[b] = t
-            engine_copy(out=stage_1[b][:, i, :], in_=banks["o1", b, i][:, :E])
+            engine_copy(out=stage(b, i // PACK)[:, i % PACK, :], in_=banks["o1", b, i][:, :E])
+
+        def open_t(b, h):
+            bank = ps_o.tile([E, BANK], F32, tag="o", name="bank_p")
+            banks["ot", b, h] = bank
+
+        def multiply_t(b, h, g):
+            c, e = dsb_codes[b, g]
+            mine = slice((PASSES + g) * E, (PASSES + g + 1) * E)
+            cols = slice(h * BANK, (h + 1) * BANK)
+            nc.tensor.matmul_mx(
+                out=banks["ot", b, h][:],
+                lhsT=kq_codes[b][:, mine].bitcast(E4M3),
+                lhsT_scale=kq_scales[b][:, mine],
+                rhs=c[:, cols].bitcast(E5M2),
+                rhs_scale=e[:, cols],
+                start=(g == 0),
+                stop=(g == PASSES - 1),
+            )
+
+        def copy_t(b, h, engine_copy):
+            t = pool.tile([E, PACK, P], F32, tag="out_t", name="out_t", bufs=2)
+            engine_copy(out=t[:], in_=banks["ot", b, h][:].rearrange("e (p i) -> e i p", i=PACK))
+            turned["ot", b, h] = t
+
+        def turn_t(b, h):
+            bank = ps_tr.tile([P, PACK, E], F32, tag="tr", name="bank_u")
+            for i in range(PACK):
+                nc.tensor.transpose(bank[:, i, :], turned["ot", b, h][:, i, :], ident[:])
+            banks["u", b, h] = bank
+
+        def copy_u(b, h, engine_copy):
+            engine_copy(out=stage(b, h)[:], in_=banks["u", b, h][:])
 
         def store_0(b, g):
             nc.sync.dma_start(
                 out=out_0[b, g * PASS : (g + 1) * PASS, :].rearrange("(p j) e -> p j e", j=PACK), in_=stage_0[b, g][:]
             )
 
-        def store_1(b, first, last):
-            nc.sync.dma_start(
-                out=out_1[b, first * P : last * P, :].rearrange("(i p) e -> p i e", p=P), in_=stage_1[b][:, first:last, :]
-            )
+        def store_1(b, h, layout):
+            view = out_1[b, h * BANK : (h + 1) * BANK, :].rearrange(layout, i=PACK)
+            nc.sync.dma_start(out=view, in_=stage_1[b, h][:])
 
         chunks = L // Q_COLS
 
         def load_for(s):
             if s == 0:
+                load_ug(0)
                 for c in range(chunks):
                     load_v(0, c)
-                load_ug(0)
                 load_mask(0)
-                load_ug(1)
-                load_kq(0)
+            load_scores(s, 2 if s == STEPS - 1 else 1)
             if s + 1 < STEPS:
                 load_mask(s + 1)
-            load_scores(s, 2 if s == STEPS - 1 else 1)
+            if s == 0:
+                load_ug(1)
+            if s % 2 == 1 and s // 2 + 2 < STEPS // 2:
+                load_ug(s // 2 + 2)
+            if 1 <= s < 1 + B:
+                load_kq(s - 1)
             if 2 <= s < 2 + chunks:
                 load_v(1, s - 2)
-            if s == 6:
-                load_kq(1)
-            if s % 2 == 0 and s // 2 + 2 < STEPS // 2:
-                load_ug(s // 2 + 2)
 
+        last = STEPS - 1
         load_for(0)
-        for c in range(chunks):
-            turn_v(0, c)
-            copy_v(0, c)
-            quant_v(0, c)
-
-        for i in range(-3, STEPS):
-            if 0 < i + 3 < STEPS:
+        for i in range(-2, last):
+            if i + 3 < STEPS:
                 load_for(i + 3)
             if i == STEPS - 2:
                 store_0(0, 0)
                 store_0(0, 1)
-                store_1(0, 0, L // P)
-                store_0(1, 0)
-
-            back_b, back_g, quarter = place(i - PACK) if i >= PACK else (0, 0, 0)
-
-            if 0 <= i + 1 < STEPS:
-                show(i + 1)
-            if i >= 2:
-                copy_0(i - 2)
-            if STEPS_B < i <= STEPS_B + QUARTERS:
-                for n in range(2):
-                    copy_1(0, 2 * (i - 1 - STEPS_B) + n, nc.scalar.copy)
-            if i >= PACK:
-                interleave(back_b, back_g, quarter, nc.scalar.copy)
 
             if i >= 0:
                 weigh(i)
                 grad_s(i)
+            if i + 2 < STEPS:
+                product(i + 2)
             if 4 <= i < 4 + chunks:
                 quant_v(1, i - 4)
 
+            if i >= 2:
+                multiply_0(i - 2)
+            if i in (11, 13):
+                h = (i - 11) // 2
+                open_t(0, h)
+                for g in range(PASSES):
+                    multiply_t(0, h, g)
+
+            if i == last - 1:
+                show(last)
+                divide(last)
+            if i >= 3:
+                copy_0(i - 3)
+            if i in (12, 14):
+                copy_t(0, (i - 12) // 2, nc.scalar.copy)
+            if i >= PACK:
+                b, g, quarter = place(i - PACK)
+                interleave(b, g, quarter, nc.scalar.copy)
+            if i == -1:
+                for c in range(chunks):
+                    turn_v(0, c)
+                    copy_v(0, c, nc.vector.tensor_copy)
+                    quant_v(0, c)
+            if -1 <= i < last - 1:
+                show(i + 1)
+                divide(i + 1)
             if i >= 0:
                 b, g, j = place(i)
                 turn_rows("ds", i, dS[b, g][:, j, :])
                 copy_rows("ds", i)
-            if 0 <= i + 2 < STEPS:
+            if i in (12, 14):
+                turn_t(0, (i - 12) // 2)
+            if i + 2 < STEPS:
                 turn_rows("dz", i + 2, dz[i + 2][:])
                 copy_rows("dz", i + 2)
+            if i == 12:
+                copy_u(0, 0, nc.scalar.copy)
             if 3 <= i < 3 + chunks:
                 turn_v(1, i - 3)
-                copy_v(1, i - 3)
+                copy_v(1, i - 3, nc.scalar.copy)
 
-            if 0 <= i + 1 < STEPS:
+            if -1 <= i < last:
                 quant_rows("dz", i + 1)
                 multiply_a(i + 1)
-            if i >= 1:
+            if 1 <= i < last:
                 quant_rows("ds", i - 1)
-                multiply_0(i - 1)
-            if i >= PACK:
-                quant_b(back_b, back_g, quarter)
-            if STEPS_B <= i < STEPS_B + QUARTERS:
-                for n in range(2):
-                    multiply_1(0, 2 * (i - STEPS_B) + n, ps_o, "o")
-            if 0 <= i + 1 < STEPS:
-                factor_1(i + 1)
-            if 0 <= i + 3 < STEPS:
-                product(i + 3)
-            if 0 <= i + 1 < STEPS:
-                factor_2(i + 1)
-            if i == -1:
-                prep_kq(0)
-            if i == STEPS_B - 1:
-                prep_kq(1)
+            if PACK < i < last:
+                quant_b(*place(i - 1 - PACK))
+            if -1 <= i < last:
+                invert(i + 1)
+            if 1 <= i < 1 + B:
+                prep_kq(i - 1)
 
-        last = STEPS - 1
-        copy_0(last - 1)
+        weigh(last)
+        grad_s(last)
+        multiply_0(last - 2)
+        copy_0(last - 3)
+        store_0(1, 0)
+        store_1(0, 0, "(p i) e -> p i e")
+        interleave(1, 0, 3, nc.scalar.copy)
+        copy_u(0, 1, nc.scalar.copy)
+        store_1(0, 1, "(p i) e -> p i e")
+        copy_0(last - 2)
         interleave(1, 1, 0, nc.scalar.copy)
+        turn_rows("ds", last, dS[1, 1][:, 3, :])
+        copy_rows("ds", last)
+        quant_rows("ds", last - 1)
+        quant_b(1, 0, 2)
+        quant_b(1, 0, 3)
         interleave(1, 1, 1, nc.vector.tensor_copy)
-        quant_b(1, 1, 0)
         interleave(1, 1, 2, nc.vector.tensor_copy)
+        multiply_0(last - 1)
+        copy_0(last - 1)
         interleave(1, 1, 3, nc.scalar.copy)
+        open_t(1, 0)
+        multiply_t(1, 0, 0)
+        for i in range(4, 8):
+            open_1(1, i, ps_da if i < 6 else ps_tr, "da" if i < 6 else "tr")
+            multiply_1(1, i, 0)
+        quant_b(1, 1, 0)
         quant_b(1, 1, 1)
-        quant_rows("ds", last)
         quant_b(1, 1, 2)
+        quant_rows("ds", last)
         quant_b(1, 1, 3)
-        for i in range(4):
-            multiply_1(1, i, ps_o if i < 2 else ps_da, "o" if i < 2 else "da")
+        multiply_t(1, 0, 1)
+        copy_t(1, 0, nc.scalar.copy)
+        for i in range(4, 6):
+            multiply_1(1, i, 1)
+            copy_1(1, i, nc.vector.tensor_copy)
         multiply_0(last)
-        for i in range(4):
-            copy_1(1, i, nc.scalar.copy if i % 2 else nc.vector.tensor_copy)
         copy_0(last)
         store_0(1, 1)
-        store_1(1, 0, 4)
-        for i in range(4, 8):
-            multiply_1(1, i, ps_o if i < 6 else ps_da, "o" if i < 6 else "da")
-            copy_1(1, i, nc.scalar.copy if i % 2 else nc.vector.tensor_copy)
-        store_1(1, 4, 8)
+        turn_t(1, 0)
+        copy_u(1, 0, nc.scalar.copy)
+        store_1(1, 0, "(p i) e -> p i e")
+        for i in range(6, 8):
+            multiply_1(1, i, 1)
+            copy_1(1, i, nc.vector.tensor_copy)
+        store_1(1, 1, "(i p) e -> p i e")

from contextlib import ExitStack

import concourse.mybir as mybir
from concourse.masks import make_identity

B, L, E, DV = 2, 1024, 128, 1024
FLOPS = 2 * B * L * L * DV + 2 * 2 * B * L * L * E

F32 = mybir.dt.float32
BF16 = mybir.dt.bfloat16
I32 = mybir.dt.int32
U32 = mybir.dt.uint32
U8 = mybir.dt.uint8
E4M3 = mybir.dt.float8_e4m3fn_x4
E5M2 = mybir.dt.float8_e5m2_x4
ALU = mybir.AluOpType
ACT = mybir.ActivationFunctionType

P = 128
PACK = 4
PASS = P * PACK
PASSES = L // PASS
BANK = 512
STEPS = B * L // P
STEPS_B = L // P
Q_COLS = 256
QUARTERS = L // Q_COLS
KQ_BLOCKS = 7


def tile_gateattention_v_kernel(tc, u, q, k, v, attn_mask, scores, grad_out, out_0, out_1):
    nc = tc.nc
    mask_words = attn_mask.bitcast(I32)

    with ExitStack() as ctx:
        ctx.enter_context(tc.manual_schedule())
        keep = ctx.enter_context(tc.tile_pool(name="keep", bufs=1))
        pool = ctx.enter_context(tc.tile_pool(name="work", bufs=2))
        ps_tr = ctx.enter_context(tc.psum_pool(name="ps_tr", bufs=3))
        ps_da = ctx.enter_context(tc.psum_pool(name="ps_da", bufs=2))
        ps_o = ctx.enter_context(tc.psum_pool(name="ps_o", bufs=3))

        ident = keep.tile([P, P], F32, name="ident")
        make_identity(nc, ident[:])
        count = keep.tile([P, STEPS], F32, name="count")
        divisor = keep.tile([P, STEPS], F32, name="divisor")
        factor = keep.tile([P, STEPS], F32, name="factor")

        v_codes, v_scales, kq_codes, kq_scales = {}, {}, {}, {}
        for b in range(B):
            v_codes[b] = keep.tile([P, PASSES, L], U32, name="v_codes" + str(b), align_bytes=64)
            v_scales[b] = keep.tile([P, PASSES, L], U8, name="v_scales" + str(b), align_bytes=64)
            kq_codes[b] = keep.tile([P, KQ_BLOCKS * E], U32, name="kq_codes" + str(b), align_bytes=64)
            kq_scales[b] = keep.tile([P, KQ_BLOCKS * E], U8, name="kq_scales" + str(b), align_bytes=64)
            nc.gpsimd.memset(kq_codes[b][:, 4 * E :], 0)
            nc.gpsimd.memset(kq_scales[b][:, 4 * E :], 0)

        v_raw, u_raw, g_raw, kq_raw, mask_raw, s_raw = {}, {}, {}, {}, {}, {}
        dz, dz_codes, shown, weight, dS = {}, {}, {}, {}, {}
        vt, turned, dsb_codes, stage_0, stage_1, banks = {}, {}, {}, {}, {}, {}

        def place(s):
            b, r = divmod(s, STEPS_B)
            g, j = divmod(r, PACK)
            return b, g, j

        def rows_of(x, s):
            b, g, j = place(s)
            return x[b, g * PASS : (g + 1) * PASS, :].rearrange("(p j) c -> p j c", j=PACK)

        def load_v(b, c):
            t = pool.tile([P, 2, DV], BF16, tag="v_raw", name="v_raw", bufs=4)
            nc.sync.dma_start(out=t[:], in_=v[b, c * Q_COLS : (c + 1) * Q_COLS, :].rearrange("(p a) d -> p a d", a=2))
            v_raw[b, c] = t

        def load_ug(pair):
            s = 2 * pair
            b, g, j = place(s)
            tg = pool.tile([P, 2, DV], BF16, tag="g_raw", name="g_raw", bufs=3)
            nc.sync.dma_start(out=tg[:], in_=rows_of(grad_out, s)[:, j : j + 2, :])
            tu = pool.tile([P, 2, DV], BF16, tag="u_raw", name="u_raw", bufs=3)
            nc.sync.dma_start(out=tu[:], in_=rows_of(u, s)[:, j : j + 2, :])
            g_raw[pair], u_raw[pair] = tg, tu

        def load_kq(b):
            tk = pool.tile([P, PASSES, PACK, E], BF16, tag="k_raw", name="k_raw", bufs=1)
            nc.sync.dma_start(out=tk[:], in_=k[b].rearrange("(g p j) e -> p g j e", p=P, j=PACK))
            tq = pool.tile([P, PASSES, PACK, E], BF16, tag="q_raw", name="q_raw", bufs=1)
            nc.sync.dma_start(out=tq[:], in_=q[b].rearrange("(g p j) e -> p g j e", p=P, j=PACK))
            kq_raw[b] = (tk, tq)

        def load_mask(s):
            j = place(s)[2]
            t = pool.tile([P, 2 * L], I32, tag="mask", name="mask", bufs=4)
            nc.sync.dma_start(out=t[:], in_=rows_of(mask_words, s)[:, j, :])
            mask_raw[s] = t

        def load_scores(s, pieces):
            j = place(s)[2]
            t = pool.tile([P, L], F32, tag="scores", name="scores", bufs=4)
            n = L // pieces
            for h in range(pieces):
                nc.sync.dma_start(out=t[:, h * n : (h + 1) * n], in_=rows_of(scores, s)[:, j, h * n : (h + 1) * n])
            s_raw[s] = t

        def turn_v(b, c):
            words = v_raw[b, c][:].bitcast(F32)
            for g in range(PASSES):
                bank = ps_tr.tile([P, 2, 2, P], F32, tag="tr", name="bank_v")
                for w in range(2):
                    for a in range(2):
                        nc.tensor.transpose(bank[:, w, a, :], words[:, a, 2 * P * g + w : 2 * P * (g + 1) : 2], ident[:])
                banks["v", b, c, g] = bank

        def copy_v(b, c, second_copy):
            for g in range(PASSES):
                t = pool.tile([P, PACK * Q_COLS], BF16, tag="turned", name="vt", bufs=6, align_bytes=64)
                engine_copy = second_copy if g else nc.scalar.copy
                engine_copy(
                    out=t[:].bitcast(F32).rearrange("p (r a w) -> p r a w", a=2, w=2),
                    in_=banks["v", b, c, g][:].rearrange("p w a r -> p r a w"),
                )
                vt[b, c, g] = t

        def quant_v(b, c):
            cols = slice(c * Q_COLS, (c + 1) * Q_COLS)
            for g in range(PASSES):
                nc.vector.quantize_mx(out=v_codes[b][:, g, cols].bitcast(E4M3), scales=v_scales[b][:, g, cols], in_=vt[b, c, g][:])

        def prep_kq(b):
            parts = []
            for raw in kq_raw[b]:
                t = pool.tile([P, PACK * Q_COLS], BF16, tag="turned", name="kqt", bufs=6, align_bytes=64)
                nc.vector.tensor_copy(
                    out=t[:].rearrange("p (g e j) -> p g e j", g=PASSES, j=PACK), in_=raw[:].rearrange("p g j e -> p g e j")
                )
                parts.append(t)
            for i, t in enumerate(parts):
                cols = slice(i * PASSES * E, (i + 1) * PASSES * E)
                nc.vector.quantize_mx(out=kq_codes[b][:, cols].bitcast(E4M3), scales=kq_scales[b][:, cols], in_=t[:])

        def product(s):
            jj = s % 2
            t = pool.tile([P, DV], BF16, tag="dz", name="dz", bufs=3)
            nc.vector.tensor_tensor(out=t[:], in0=g_raw[s // 2][:, jj, :], in1=u_raw[s // 2][:, jj, :], op=ALU.mult)
            dz[s] = t

        def turn_rows(kind, s, tile):
            words = tile.bitcast(F32)
            bank = ps_tr.tile([P, PASSES, 2, P], F32, tag="tr", name="bank_t")
            for g in range(PASSES):
                for w in range(2):
                    nc.tensor.transpose(bank[:, g, w, :], words[:, 2 * P * g + w : 2 * P * (g + 1) : 2], ident[:])
            banks[kind, s] = bank

        def copy_rows(kind, s):
            t = pool.tile([P, PACK * Q_COLS], BF16, tag="turned", name="rt", bufs=6, align_bytes=64)
            nc.scalar.copy(
                out=t[:].bitcast(F32).rearrange("p (g r w) -> p g r w", g=PASSES, w=2),
                in_=banks[kind, s][:].rearrange("p g w r -> p g r w"),
            )
            turned[kind, s] = t

        def quant_rows(kind, s):
            c = pool.tile([P, PASSES * P], U32, tag="rows_codes", name="rows_codes", bufs=5, align_bytes=64)
            e = pool.tile([P, PASSES * P], U8, tag="rows_scales", name="rows_scales", bufs=5, align_bytes=64)
            nc.vector.quantize_mx(out=c[:].bitcast(E5M2), scales=e[:], in_=turned[kind, s][:])
            dz_codes[kind, s] = (c, e)

        def multiply_a(s):
            b = place(s)[0]
            c, e = dz_codes["dz", s]
            for h in range(L // BANK):
                bank = ps_da.tile([P, BANK], F32, tag="da", name="bank_a")
                cols = slice(h * BANK, (h + 1) * BANK)
                for g in range(PASSES):
                    mine = slice(g * P, (g + 1) * P)
                    nc.tensor.matmul_mx(
                        out=bank[:],
                        lhsT=c[:, mine].bitcast(E5M2),
                        lhsT_scale=e[:, mine],
                        rhs=v_codes[b][:, g, cols].bitcast(E4M3),
                        rhs_scale=v_scales[b][:, g, cols],
                        start=(g == 0),
                        stop=(g == PASSES - 1),
                    )
                banks["da", s, h] = bank

        def show(s):
            t = pool.tile([P, L], BF16, tag="shown", name="shown", bufs=3)
            low = mask_raw[s][:].bitcast(U32).rearrange("p (n w) -> p n w", w=2)[:, :, 0]
            nc.scalar.activation(out=t[:], in_=low, func=ACT.Copy, scale=-1.0, bias=1.0, accum_out=count[:, s : s + 1])
            shown[s] = t

        def divide(s):
            cols = slice(s, s + 1)
            nc.gpsimd.tensor_scalar(out=divisor[:, cols], in0=count[:, cols], scalar1=1.0, scalar2=64.0, op0=ALU.max, op1=ALU.mult)

        def invert(s):
            cols = slice(s, s + 1)
            nc.vector.reciprocal(out=factor[:, cols], in_=divisor[:, cols])

        def weigh(s):
            t = pool.tile([P, L], F32, tag="weight", name="weight", bufs=2)
            for h in range(L // BANK):
                cols = slice(h * BANK, (h + 1) * BANK)
                nc.vector.scalar_tensor_tensor(
                    out=t[:, cols], in0=s_raw[s][:, cols], scalar=0.0, in1=shown[s][:, cols], op0=ALU.max, op1=ALU.mult
                )
            weight[s] = t

        def grad_s(s):
            b, g, j = place(s)
            if j == 0:
                t = pool.tile([P, PACK, L], BF16, tag="dS", name="dS", bufs=2)
                dS[b, g] = t
            for h in range(L // BANK):
                cols = slice(h * BANK, (h + 1) * BANK)
                nc.vector.scalar_tensor_tensor(
                    out=dS[b, g][:, j, cols],
                    in0=banks["da", s, h][:],
                    scalar=factor[:, s : s + 1],
                    in1=weight[s][:, cols],
                    op0=ALU.mult,
                    op1=ALU.mult,
                )

        def multiply_0(s):
            b, gm, j = place(s)
            c, e = dz_codes["ds", s]
            bank = ps_o.tile([P, BANK], F32, tag="o", name="bank_0")
            for g in range(PASSES):
                mine = slice(g * P, (g + 1) * P)
                cols = slice(g * E, g * E + BANK)
                nc.tensor.matmul_mx(
                    out=bank[:],
                    lhsT=c[:, mine].bitcast(E5M2),
                    lhsT_scale=e[:, mine],
                    rhs=kq_codes[b][:, cols].bitcast(E4M3),
                    rhs_scale=kq_scales[b][:, cols],
                    start=(g == 0),
                    stop=(g == PASSES - 1),
                )
            banks["o0", s] = bank

        def copy_0(s):
            b, g, j = place(s)
            if j == 0:
                t = pool.tile([P, PACK, E], F32, tag="stage_0", name="stage_0", bufs=4)
                stage_0[b, g] = t
            nc.scalar.copy(out=stage_0[b, g][:, j, :], in_=banks["o0", s][:, :E])

        def interleave(b, g, quarter, engine_copy):
            t = pool.tile([P, Q_COLS, PACK], BF16, tag="inter", name="inter", bufs=4, align_bytes=64)
            cols = slice(quarter * Q_COLS, (quarter + 1) * Q_COLS)
            engine_copy(
                out=t[:].rearrange("p (c i) t -> p c t i", i=4),
                in_=dS[b, g][:, :, cols].rearrange("p t (c i) -> p c t i", i=4),
            )
            turned["b", b, g, quarter] = t

        def quant_b(b, g, quarter):
            if quarter == 0:
                c = pool.tile([P, L], U32, tag="dsb_codes", name="dsb_codes", bufs=3, align_bytes=64)
                e = pool.tile([P, L], U8, tag="dsb_scales", name="dsb_scales", bufs=3, align_bytes=64)
                dsb_codes[b, g] = (c, e)
            c, e = dsb_codes[b, g]
            cols = slice(quarter * Q_COLS, (quarter + 1) * Q_COLS)
            nc.vector.quantize_mx(
                out=c[:, cols].bitcast(E5M2), scales=e[:, cols], in_=turned["b", b, g, quarter][:].rearrange("p n t -> p (n t)")
            )

        def open_1(b, i, psum, tag):
            bank = psum.tile([P, BANK], F32, tag=tag, name="bank_1")
            banks["o1", b, i] = bank

        def multiply_1(b, i, g):
            mine = slice(i * P, (i + 1) * P)
            c, e = dsb_codes[b, g]
            cols = slice((PASSES + g) * E, (PASSES + g) * E + BANK)
            nc.tensor.matmul_mx(
                out=banks["o1", b, i][:],
                lhsT=c[:, mine].bitcast(E5M2),
                lhsT_scale=e[:, mine],
                rhs=kq_codes[b][:, cols].bitcast(E4M3),
                rhs_scale=kq_scales[b][:, cols],
                start=(g == 0),
                stop=(g == PASSES - 1),
            )

        def stage(b, h):
            if (b, h) not in stage_1:
                t = pool.tile([P, PACK, E], F32, tag="stage_1", name="stage_1", bufs=4)
                stage_1[b, h] = t
            return stage_1[b, h]

        def copy_1(b, i, engine_copy):
            engine_copy(out=stage(b, i // PACK)[:, i % PACK, :], in_=banks["o1", b, i][:, :E])

        def open_t(b, h):
            bank = ps_o.tile([E, BANK], F32, tag="o", name="bank_p")
            banks["ot", b, h] = bank

        def multiply_t(b, h, g):
            c, e = dsb_codes[b, g]
            mine = slice((PASSES + g) * E, (PASSES + g + 1) * E)
            cols = slice(h * BANK, (h + 1) * BANK)
            nc.tensor.matmul_mx(
                out=banks["ot", b, h][:],
                lhsT=kq_codes[b][:, mine].bitcast(E4M3),
                lhsT_scale=kq_scales[b][:, mine],
                rhs=c[:, cols].bitcast(E5M2),
                rhs_scale=e[:, cols],
                start=(g == 0),
                stop=(g == PASSES - 1),
            )

        def copy_t(b, h, engine_copy):
            t = pool.tile([E, PACK, P], F32, tag="out_t", name="out_t", bufs=2)
            engine_copy(out=t[:], in_=banks["ot", b, h][:].rearrange("e (p i) -> e i p", i=PACK))
            turned["ot", b, h] = t

        def turn_t(b, h):
            bank = ps_tr.tile([P, PACK, E], F32, tag="tr", name="bank_u")
            for i in range(PACK):
                nc.tensor.transpose(bank[:, i, :], turned["ot", b, h][:, i, :], ident[:])
            banks["u", b, h] = bank

        def copy_u(b, h, engine_copy):
            engine_copy(out=stage(b, h)[:], in_=banks["u", b, h][:])

        def store_0(b, g):
            nc.sync.dma_start(
                out=out_0[b, g * PASS : (g + 1) * PASS, :].rearrange("(p j) e -> p j e", j=PACK), in_=stage_0[b, g][:]
            )

        def store_1(b, h, layout):
            view = out_1[b, h * BANK : (h + 1) * BANK, :].rearrange(layout, i=PACK)
            nc.sync.dma_start(out=view, in_=stage_1[b, h][:])

        chunks = L // Q_COLS

        def load_for(s):
            if s == 0:
                load_ug(0)
                for c in range(chunks):
                    load_v(0, c)
                load_mask(0)
            load_scores(s, 2 if s == STEPS - 1 else 1)
            if s + 1 < STEPS:
                load_mask(s + 1)
            if s == 0:
                load_ug(1)
            if s % 2 == 1 and s // 2 + 2 < STEPS // 2:
                load_ug(s // 2 + 2)
            if 1 <= s < 1 + B:
                load_kq(s - 1)
            if 2 <= s < 2 + chunks:
                load_v(1, s - 2)

        last = STEPS - 1
        load_for(0)
        for i in range(-2, last):
            if i + 3 < STEPS:
                load_for(i + 3)
            if i == STEPS - 2:
                store_0(0, 0)
                store_0(0, 1)

            if i >= 0:
                weigh(i)
                grad_s(i)
            if i + 2 < STEPS:
                product(i + 2)
            if 4 <= i < 4 + chunks:
                quant_v(1, i - 4)

            if i >= 2:
                multiply_0(i - 2)
            if i in (11, 13):
                h = (i - 11) // 2
                open_t(0, h)
                for g in range(PASSES):
                    multiply_t(0, h, g)

            if i == last - 1:
                show(last)
                divide(last)
            if i >= 3:
                copy_0(i - 3)
            if i in (12, 14):
                copy_t(0, (i - 12) // 2, nc.scalar.copy)
            if i >= PACK:
                b, g, quarter = place(i - PACK)
                interleave(b, g, quarter, nc.scalar.copy)
            if i == -1:
                for c in range(chunks):
                    turn_v(0, c)
                    copy_v(0, c, nc.vector.tensor_copy)
                    quant_v(0, c)
            if -1 <= i < last - 1:
                show(i + 1)
                divide(i + 1)
            if i >= 0:
                b, g, j = place(i)
                turn_rows("ds", i, dS[b, g][:, j, :])
                copy_rows("ds", i)
            if i in (12, 14):
                turn_t(0, (i - 12) // 2)
            if i + 2 < STEPS:
                turn_rows("dz", i + 2, dz[i + 2][:])
                copy_rows("dz", i + 2)
            if i == 12:
                copy_u(0, 0, nc.scalar.copy)
            if 3 <= i < 3 + chunks:
                turn_v(1, i - 3)
                copy_v(1, i - 3, nc.scalar.copy)

            if -1 <= i < last:
                quant_rows("dz", i + 1)
                multiply_a(i + 1)
            if 1 <= i < last:
                quant_rows("ds", i - 1)
            if PACK < i < last:
                quant_b(*place(i - 1 - PACK))
            if -1 <= i < last:
                invert(i + 1)
            if 1 <= i < 1 + B:
                prep_kq(i - 1)

        weigh(last)
        grad_s(last)
        multiply_0(last - 2)
        copy_0(last - 3)
        store_0(1, 0)
        store_1(0, 0, "(p i) e -> p i e")
        interleave(1, 0, 3, nc.scalar.copy)
        copy_u(0, 1, nc.scalar.copy)
        store_1(0, 1, "(p i) e -> p i e")
        copy_0(last - 2)
        interleave(1, 1, 0, nc.scalar.copy)
        turn_rows("ds", last, dS[1, 1][:, 3, :])
        copy_rows("ds", last)
        quant_rows("ds", last - 1)
        quant_b(1, 0, 2)
        quant_b(1, 0, 3)
        interleave(1, 1, 1, nc.vector.tensor_copy)
        interleave(1, 1, 2, nc.vector.tensor_copy)
        multiply_0(last - 1)
        copy_0(last - 1)
        interleave(1, 1, 3, nc.scalar.copy)
        open_t(1, 0)
        multiply_t(1, 0, 0)
        for i in range(4, 8):
            open_1(1, i, ps_da if i < 6 else ps_tr, "da" if i < 6 else "tr")
            multiply_1(1, i, 0)
        quant_b(1, 1, 0)
        quant_b(1, 1, 1)
        quant_b(1, 1, 2)
        quant_rows("ds", last)
        quant_b(1, 1, 3)
        multiply_t(1, 0, 1)
        copy_t(1, 0, nc.scalar.copy)
        for i in range(4, 6):
            multiply_1(1, i, 1)
            copy_1(1, i, nc.vector.tensor_copy)
        multiply_0(last)
        copy_0(last)
        store_0(1, 1)
        turn_t(1, 0)
        copy_u(1, 0, nc.scalar.copy)
        store_1(1, 0, "(p i) e -> p i e")
        for i in range(6, 8):
            multiply_1(1, i, 1)
            copy_1(1, i, nc.vector.tensor_copy)
        store_1(1, 1, "(i p) e -> p i e")
